import numpy as np
import ml_dtypes


def mxq(x, axis, fmt="e4m3"):
    dtype, down = {"e4m3": (ml_dtypes.float8_e4m3fn, 7), "e5m2": (ml_dtypes.float8_e5m2, 14)}[fmt]
    v = np.moveaxis(np.asarray(x, np.float32).astype(ml_dtypes.bfloat16).astype(np.float64), axis, -1)
    blocks = v.reshape(v.shape[:-1] + (-1, 32))
    amax = np.abs(blocks).max(-1, keepdims=True)
    byte = np.maximum(np.where(amax > 0, np.frexp(amax)[1] - 1 + 127, 0) - down, 1)
    scale = np.exp2(byte - 127.0)
    codes = (blocks / scale).astype(np.float32).astype(dtype).astype(np.float64)
    return np.moveaxis((codes * scale).reshape(v.shape), -1, axis)


WIDE = False


def mx_kscale(k):
    if not WIDE:
        return np.ones(k)
    levels = np.array([10, -10, 5, -5, 0])
    a = np.random.permutation(np.resize(levels, k // 512 * 4)).reshape(k // 512, 4)
    idx = np.arange(k)
    return np.exp2(a[idx // 512, idx % 128 // 32])


BF16 = ml_dtypes.bfloat16


def bf(x):
    return np.asarray(x, np.float32).astype(BF16)


def f64(x):
    return np.asarray(x).astype(np.float64)


B, D, N, K = 4, 1024, 1024, 128
EPS = 1e-06


def l2_normalize(v, axis):
    nrm = np.sqrt(np.sum(v * v, axis=axis, keepdims=True))
    return v / np.maximum(nrm, EPS)


def setup_inputs():
    r = np.sqrt(D)
    u = np.exp2(np.round(np.log2(mx_kscale(N)) / 2))
    c = np.exp2(np.round(np.log2(np.mean(u * u)) / 2))
    g = 1.8 * np.random.standard_normal((B, K, N)) + 2.3 * np.random.standard_normal((B, K, 1))
    e = np.exp(g - g.max(axis=1, keepdims=True))
    probs = e / e.sum(axis=1, keepdims=True)
    x = (10.0 * np.random.standard_normal((B, D, N)) + 6.0 * np.random.standard_normal((B, D, 1))) / r
    mu = 3.5 * np.random.standard_normal((1, D, K)) / r
    sigma = 1.0 + 9.0 / r * (np.random.random((1, D, K)) - 0.5)
    return {"probs": bf(probs * (u * u)), "x": bf(x * (c / u)), "mu": bf(mu), "sigma": bf(sigma)}


def reference(probs, x, mu, sigma):
    probs, x, mu, sigma = f64(probs), f64(x), f64(mu), f64(sigma)
    probs_norm = probs / (np.sum(probs, axis=2, keepdims=True) + EPS)
    pq = mxq(probs_norm, 2, "e4m3").transpose(0, 2, 1)
    x2 = x * x
    weighted_mu = mxq(x, 2, "e4m3") @ pq
    weighted_x2 = mxq(x2, 2, "e4m3") @ pq
    sigma_hat = np.sqrt(np.maximum(weighted_x2 - weighted_mu * weighted_mu, EPS))
    feat = np.concatenate([weighted_mu - mu, sigma_hat - sigma], axis=1)
    feat = l2_normalize(feat, 1)
    feat = feat.reshape(B, -1)
    return l2_normalize(feat, 1)

@@ -1,0 +1,245 @@
+from contextlib import ExitStack
+
+import concourse.mybir as mybir
+from concourse.masks import make_identity
+
+F32 = mybir.dt.float32
+BF16 = mybir.dt.bfloat16
+U32 = mybir.dt.uint32
+U8 = mybir.dt.uint8
+FP8X4 = mybir.dt.float8_e4m3fn_x4
+ALU = mybir.AluOpType
+ACT = mybir.ActivationFunctionType
+
+B, D, N, K = 4, 1024, 1024, 128
+EPS = 1e-06
+P = 128
+T = D // P
+HALVES = 2
+TH = T // HALVES
+DH = D // HALVES
+PASSES = N // 512
+
+FLOPS = 2 * 2 * B * D * N * K
+
+
+def tile_wassvladlayer_pb_t_kernel(tc, probs, x, mu, sigma, out):
+    nc = tc.nc
+    x_view = x.rearrange("b (p t) n -> b p t n", t=T)
+    out_view = out.rearrange("b (s p t k) -> b p s t k", s=2, p=P, t=T)
+
+    with ExitStack() as ctx:
+        keep = ctx.enter_context(tc.tile_pool(name="keep", bufs=1))
+        work = ctx.enter_context(tc.tile_pool(name="work", bufs=2))
+        small = ctx.enter_context(tc.tile_pool(name="small", bufs=2))
+        psum = ctx.enter_context(tc.psum_pool(name="psum", bufs=1))
+
+        probs_sb = keep.tile([P, B, N], BF16, name="probs_sb")
+        mu_sb = keep.tile([P, T, K], BF16, name="mu_sb")
+        sigma_sb = keep.tile([P, T, K], BF16, name="sigma_sb")
+        x_sb = {}
+        for b in range(B):
+            nc.sync.dma_start(out=probs_sb[:, b, :], in_=probs[b])
+            for h in range(HALVES):
+                x_sb[(b, h)] = keep.tile([P, TH * N], BF16, name="x_sb_%d_%d" % (b, h))
+                nc.sync.dma_start(
+                    out=x_sb[(b, h)][:].rearrange("p (t n) -> p t n", t=TH),
+                    in_=x_view[b, :, h * TH : (h + 1) * TH, :],
+                )
+                if b == 0 and h == 0:
+                    nc.sync.dma_start(out=mu_sb[:], in_=mu[0].rearrange("(p t) k -> p t k", t=T))
+                    nc.sync.dma_start(out=sigma_sb[:], in_=sigma[0].rearrange("(p t) k -> p t k", t=T))
+
+        ident_f32 = keep.tile([P, P], F32, name="ident_f32")
+        make_identity(nc, ident_f32[:])
+        ident_bf16 = keep.tile([P, P], BF16, name="ident_bf16")
+        make_identity(nc, ident_bf16[:])
+        ones_f32 = keep.tile([P, P], F32, name="ones_f32")
+        nc.vector.memset(ones_f32[:], 1.0)
+        warm = keep.tile([P, 1], F32, name="warm")
+        nc.scalar.sqrt(warm[:], ones_f32[:, 0:1])
+
+        mu_t = keep.tile([P, D], BF16, name="mu_t")
+        sigma_t = keep.tile([P, D], BF16, name="sigma_t")
+        for rows, turned in ((mu_sb, mu_t), (sigma_sb, sigma_t)):
+            bank = psum.tile([P, T, P], BF16, tag="misc")
+            for t in range(T):
+                nc.tensor.transpose(bank[:, t, :], rows[:, t, :], ident_bf16[:])
+            nc.vector.tensor_copy(out=turned[:], in_=bank[:].rearrange("k t p -> k (t p)"))
+
+        p_sums = keep.tile([P, B], F32, name="p_sums")
+        p_codes = keep.tile([P, B, PASSES * K], U32, name="p_codes", align_bytes=64)
+        p_scales = keep.tile([P, B, PASSES * K], U8, name="p_scales", align_bytes=64)
+
+        def quantise_p(b):
+            unread = work.tile([P, N], BF16, tag="unread_p")
+            nc.scalar.activation(
+                out=unread[:], in_=probs_sb[:, b, :], func=ACT.Copy, accum_out=p_sums[:, b : b + 1]
+            )
+            denom = small.tile([P, 1], F32, tag="denom")
+            nc.vector.tensor_scalar_add(out=denom[:], in0=p_sums[:, b : b + 1], scalar1=EPS)
+            inv_denom = small.tile([P, 1], F32, tag="inv_denom")
+            nc.vector.reciprocal(out=inv_denom[:], in_=denom[:])
+            p_bf16 = work.tile([P, N], BF16, tag="p_bf16")
+            nc.vector.tensor_scalar_mul(out=p_bf16[:], in0=probs_sb[:, b, :], scalar1=inv_denom[:, 0:1])
+            by_word = p_bf16[:].rearrange("k (g u j e) -> k g u e j", g=PASSES, u=2, e=2)
+            bank = psum.tile([P, PASSES * 4, K], BF16, tag="misc")
+            for g in range(PASSES):
+                for u in range(2):
+                    for e in range(2):
+                        nc.tensor.transpose(bank[:, 4 * g + 2 * u + e, :], by_word[:, g, u, e, :], ident_bf16[:])
+            p_grouped = work.tile([P, PASSES * K * 4], BF16, tag="p_grouped", align_bytes=64)
+            nc.vector.tensor_copy(
+                out=p_grouped[:].rearrange("j (g k v) -> j g k v", g=PASSES, v=4),
+                in_=bank[:].rearrange("j (g v) k -> j g k v", g=PASSES),
+            )
+            nc.vector.quantize_mx(
+                out=p_codes[:, b, :].bitcast(FP8X4), scales=p_scales[:, b, :], in_=p_grouped[:]
+            )
+
+        def quantise_x(b, h):
+            words = x_sb[(b, h)][:].bitcast(F32).rearrange("p (t w) -> p t w", t=TH)
+            x_grouped = work.tile([P, PASSES * DH * 4], BF16, tag="x_grouped", align_bytes=64)
+            sq_grouped = work.tile([P, PASSES * DH * 4], BF16, tag="sq_grouped", align_bytes=64)
+            x_codes = work.tile([P, PASSES, DH], U32, tag="x_codes", align_bytes=64)
+            x_scales = work.tile([P, PASSES, DH], U8, tag="x_scales", align_bytes=64)
+            sq_codes = work.tile([P, PASSES, DH], U32, tag="sq_codes", align_bytes=64)
+            sq_scales = work.tile([P, PASSES, DH], U8, tag="sq_scales", align_bytes=64)
+            x_words = x_grouped[:].bitcast(F32).rearrange("j (g c u) -> j g c u", g=PASSES, u=2)
+            x_vals = x_grouped[:].rearrange("j (g cv) -> j g cv", g=PASSES)
+            sq_vals = sq_grouped[:].rearrange("j (g cv) -> j g cv", g=PASSES)
+            sq_pairs = sq_grouped[:].rearrange("j (g c u e) -> j g c u e", g=PASSES, u=2, e=2)
+            for g in range(PASSES):
+                for pair in range(TH // 2):
+                    bank = psum.tile([P, 512], F32, tag="xt", bufs=3)
+                    for u in range(2):
+                        for i in range(2):
+                            nc.tensor.transpose(
+                                bank[:, 256 * u + 128 * i : 256 * u + 128 * (i + 1)],
+                                words[:, 2 * pair + i, 256 * g + 128 * u : 256 * g + 128 * (u + 1)],
+                                ident_f32[:],
+                            )
+                    cols = slice(256 * pair, 256 * (pair + 1))
+                    nc.scalar.copy(
+                        out=x_words[:, g, cols, :], in_=bank[:].rearrange("j (u c) -> j c u", u=2)
+                    )
+                    if g == PASSES - 1 and pair == TH // 2 - 1:
+                        nc.scalar.activation(
+                            out=sq_pairs[:, g, cols, :, :],
+                            in_=bank[:].bitcast(BF16).rearrange("j (u c e) -> j c u e", u=2, e=2),
+                            func=ACT.Square,
+                        )
+                by_vector = 4 * DH if g < PASSES - 1 else 2 * DH
+                nc.vector.tensor_tensor(
+                    out=sq_vals[:, g, 0:by_vector],
+                    in0=x_vals[:, g, 0:by_vector],
+                    in1=x_vals[:, g, 0:by_vector],
+                    op=ALU.mult,
+                )
+                nc.vector.quantize_mx(
+                    out=x_codes[:, g, :].bitcast(FP8X4), scales=x_scales[:, g, :], in_=x_vals[:, g, :]
+                )
+                nc.vector.quantize_mx(
+                    out=sq_codes[:, g, :].bitcast(FP8X4), scales=sq_scales[:, g, :], in_=sq_vals[:, g, :]
+                )
+            return x_codes, x_scales, sq_codes, sq_scales
+
+        def moments(b, operands):
+            x_codes, x_scales, sq_codes, sq_scales = operands
+            m1 = psum.tile([P, DH], F32, tag="m1")
+            m2 = psum.tile([P, DH], F32, tag="m2")
+            for acc, codes, scales in ((m1, x_codes, x_scales), (m2, sq_codes, sq_scales)):
+                for g in range(PASSES):
+                    nc.tensor.matmul_mx(
+                        out=acc[:],
+                        lhsT=p_codes[:, b, g * K : (g + 1) * K].bitcast(FP8X4),
+                        lhsT_scale=p_scales[:, b, g * K : (g + 1) * K],
+                        rhs=codes[:, g, :].bitcast(FP8X4),
+                        rhs_scale=scales[:, g, :],
+                        start=(g == 0),
+                        stop=(g == PASSES - 1),
+                    )
+            return m1, m2
+
+        def residuals(h, m1, m2, feat, sums_sq):
+            cols = slice(h * DH, (h + 1) * DH)
+            m1_sq = work.tile([P, DH], F32, tag="m1_sq")
+            nc.scalar.activation(out=m1_sq[:], in_=m1[:], func=ACT.Square)
+            nc.vector.tensor_tensor(out=feat[:, 0, cols], in0=m1[:], in1=mu_t[:, cols], op=ALU.subtract)
+            var = work.tile([P, DH], F32, tag="var")
+            nc.vector.tensor_tensor(out=var[:], in0=m2[:], in1=m1_sq[:], op=ALU.subtract)
+            nc.vector.tensor_scalar_max(out=var[:], in0=var[:], scalar1=EPS)
+            std = work.tile([P, DH], F32, tag="std")
+            nc.scalar.activation(out=std[:], in_=var[:], func=ACT.Sqrt)
+            nc.vector.tensor_tensor(out=feat[:, 1, cols], in0=std[:], in1=sigma_t[:, cols], op=ALU.subtract)
+            for s in range(2):
+                unread = work.tile([P, DH], BF16, tag="unread_sq", bufs=4)
+                nc.scalar.activation(
+                    out=unread[:],
+                    in_=feat[:, s, cols],
+                    func=ACT.Square,
+                    accum_out=sums_sq[:, 2 * h + s : 2 * h + s + 1],
+                )
+
+        def inv_sqrt_floor(value, tag):
+            floored = small.tile([P, 1], F32, tag=tag + "_floored")
+            nc.vector.tensor_scalar_max(out=floored[:], in0=value, scalar1=EPS * EPS)
+            root = small.tile([P, 1], F32, tag=tag + "_root")
+            nc.scalar.activation(out=root[:], in_=floored[:], func=ACT.Sqrt)
+            inv = small.tile([P, 1], F32, tag=tag + "_inv")
+            nc.vector.reciprocal(out=inv[:], in_=root[:])
+            return inv
+
+        def normalise_and_store(b, feat, sums_sq):
+            col_sq = small.tile([P, 1], F32, tag="col_sq")
+            nc.vector.tensor_reduce(out=col_sq[:], in_=sums_sq[:], axis=mybir.AxisListType.X, op=ALU.add)
+            inv_col = inv_sqrt_floor(col_sq[:], "col")
+            left_sq = small.tile([P, 1], F32, tag="left_sq")
+            nc.vector.tensor_scalar(
+                out=left_sq[:], in0=col_sq[:], scalar1=inv_col[:, 0:1], scalar2=inv_col[:, 0:1],
+                op0=ALU.mult, op1=ALU.mult,
+            )
+            spread = psum.tile([P, 2, P], F32, tag="misc")
+            nc.tensor.matmul(
+                out=spread[:, 0, :], lhsT=inv_col[:, 0:1].to_broadcast([P, P]), rhs=ident_f32[:],
+                start=True, stop=True,
+            )
+            nc.tensor.matmul(
+                out=spread[:, 1, :], lhsT=left_sq[:, 0:1].to_broadcast([P, P]), rhs=ones_f32[:],
+                start=True, stop=True,
+            )
+            inv_all = inv_sqrt_floor(spread[:, 1, 0:1], "all")
+            factor = small.tile([P, K], F32, tag="factor")
+            nc.vector.tensor_scalar_mul(out=factor[:], in0=spread[:, 0, :], scalar1=inv_all[:, 0:1])
+            result = work.tile([P, 2, T, K], F32, tag="result")
+            for s in range(2):
+                for h in range(HALVES):
+                    bank = psum.tile([P, TH, K], F32, tag="ot", bufs=2)
+                    for i in range(TH):
+                        t = h * TH + i
+                        nc.tensor.transpose(bank[:, i, :], feat[:, s, t * P : (t + 1) * P], ident_f32[:])
+                    nc.vector.tensor_tensor(
+                        out=result[:, s, h * TH : (h + 1) * TH, :],
+                        in0=bank[:],
+                        in1=factor[:].unsqueeze(1).to_broadcast([P, TH, K]),
+                        op=ALU.mult,
+                    )
+            nc.sync.dma_start(out=out_view[b], in_=result[:])
+
+        units = [(b, h) for b in range(B) for h in range(HALVES)]
+        quantise_p(0)
+        operands = {units[0]: quantise_x(0, 0)}
+        feat = None
+        sums_sq = None
+        for i, (b, h) in enumerate(units):
+            if i + 1 < len(units):
+                if units[i + 1][1] == 0:
+                    quantise_p(units[i + 1][0])
+                operands[units[i + 1]] = quantise_x(units[i + 1][0], units[i + 1][1])
+            if h == 0:
+                feat = work.tile([P, 2, D], F32, tag="feat")
+                sums_sq = small.tile([P, 2 * HALVES], F32, tag="sums_sq")
+            m1, m2 = moments(b, operands[(b, h)])
+            residuals(h, m1, m2, feat, sums_sq)
+            if h == HALVES - 1:
+                normalise_and_store(b, feat, sums_sq)

@@ -16,9 +16,12 @@ EPS = 1e-06
 P = 128
 T = D // P
 HALVES = 2
+UNITS = B * HALVES
 TH = T // HALVES
 DH = D // HALVES
 PASSES = N // 512
+LAG = 3
+TURN_LAG = LAG + 4
 
 FLOPS = 2 * 2 * B * D * N * K
 
@@ -26,29 +29,31 @@ FLOPS = 2 * 2 * B * D * N * K
 def tile_wassvladlayer_pb_t_kernel(tc, probs, x, mu, sigma, out):
     nc = tc.nc
     x_view = x.rearrange("b (p t) n -> b p t n", t=T)
-    out_view = out.rearrange("b (s p t k) -> b p s t k", s=2, p=P, t=T)
+    out_view = out.rearrange("b (s p t k) -> b s p t k", s=2, p=P, t=T)
 
     with ExitStack() as ctx:
         keep = ctx.enter_context(tc.tile_pool(name="keep", bufs=1))
         work = ctx.enter_context(tc.tile_pool(name="work", bufs=2))
-        small = ctx.enter_context(tc.tile_pool(name="small", bufs=2))
+        small = ctx.enter_context(tc.tile_pool(name="small", bufs=3))
         psum = ctx.enter_context(tc.psum_pool(name="psum", bufs=1))
 
         probs_sb = keep.tile([P, B, N], BF16, name="probs_sb")
-        mu_sb = keep.tile([P, T, K], BF16, name="mu_sb")
-        sigma_sb = keep.tile([P, T, K], BF16, name="sigma_sb")
-        x_sb = {}
         for b in range(B):
             nc.sync.dma_start(out=probs_sb[:, b, :], in_=probs[b])
-            for h in range(HALVES):
-                x_sb[(b, h)] = keep.tile([P, TH * N], BF16, name="x_sb_%d_%d" % (b, h))
+        mu_sb = keep.tile([P, T, K], BF16, name="mu_sb")
+        sigma_sb = keep.tile([P, T, K], BF16, name="sigma_sb")
+        x_raw = {}
+        for u in range(UNITS):
+            b, h = divmod(u, HALVES)
+            x_raw[u] = keep.tile([P, TH * N], BF16, name="x_raw_%d" % u)
+            for pair in range(TH // 2):
                 nc.sync.dma_start(
-                    out=x_sb[(b, h)][:].rearrange("p (t n) -> p t n", t=TH),
-                    in_=x_view[b, :, h * TH : (h + 1) * TH, :],
+                    out=x_raw[u][:, 2 * pair * N : 2 * (pair + 1) * N].rearrange("p (t n) -> p t n", t=2),
+                    in_=x_view[b, :, h * TH + 2 * pair : h * TH + 2 * (pair + 1), :],
                 )
-                if b == 0 and h == 0:
-                    nc.sync.dma_start(out=mu_sb[:], in_=mu[0].rearrange("(p t) k -> p t k", t=T))
-                    nc.sync.dma_start(out=sigma_sb[:], in_=sigma[0].rearrange("(p t) k -> p t k", t=T))
+            if u == 0:
+                nc.sync.dma_start(out=mu_sb[:], in_=mu[0].rearrange("(p t) k -> p t k", t=T))
+                nc.sync.dma_start(out=sigma_sb[:], in_=sigma[0].rearrange("(p t) k -> p t k", t=T))
 
         ident_f32 = keep.tile([P, P], F32, name="ident_f32")
         make_identity(nc, ident_f32[:])
@@ -56,22 +61,17 @@ def tile_wassvladlayer_pb_t_kernel(tc, probs, x, mu, sigma, out):
         make_identity(nc, ident_bf16[:])
         ones_f32 = keep.tile([P, P], F32, name="ones_f32")
         nc.vector.memset(ones_f32[:], 1.0)
+        minus_half = keep.tile([P, 1], F32, name="minus_half")
+        nc.vector.memset(minus_half[:], -0.5)
         warm = keep.tile([P, 1], F32, name="warm")
         nc.scalar.sqrt(warm[:], ones_f32[:, 0:1])
-
-        mu_t = keep.tile([P, D], BF16, name="mu_t")
-        sigma_t = keep.tile([P, D], BF16, name="sigma_t")
-        for rows, turned in ((mu_sb, mu_t), (sigma_sb, sigma_t)):
-            bank = psum.tile([P, T, P], BF16, tag="misc")
-            for t in range(T):
-                nc.tensor.transpose(bank[:, t, :], rows[:, t, :], ident_bf16[:])
-            nc.vector.tensor_copy(out=turned[:], in_=bank[:].rearrange("k t p -> k (t p)"))
 
         p_sums = keep.tile([P, B], F32, name="p_sums")
         p_codes = keep.tile([P, B, PASSES * K], U32, name="p_codes", align_bytes=64)
         p_scales = keep.tile([P, B, PASSES * K], U8, name="p_scales", align_bytes=64)
+        p_banks = {}
 
-        def quantise_p(b):
+        def normalise_p(b):
             unread = work.tile([P, N], BF16, tag="unread_p")
             nc.scalar.activation(
                 out=unread[:], in_=probs_sb[:, b, :], func=ACT.Copy, accum_out=p_sums[:, b : b + 1]
@@ -83,69 +83,114 @@ def tile_wassvladlayer_pb_t_kernel(tc, probs, x, mu, sigma, out):
             p_bf16 = work.tile([P, N], BF16, tag="p_bf16")
             nc.vector.tensor_scalar_mul(out=p_bf16[:], in0=probs_sb[:, b, :], scalar1=inv_denom[:, 0:1])
             by_word = p_bf16[:].rearrange("k (g u j e) -> k g u e j", g=PASSES, u=2, e=2)
-            bank = psum.tile([P, PASSES * 4, K], BF16, tag="misc")
+            bank = psum.tile([P, PASSES * 4, K], BF16, tag="ot", bufs=2)
             for g in range(PASSES):
-                for u in range(2):
+                for half in range(2):
                     for e in range(2):
-                        nc.tensor.transpose(bank[:, 4 * g + 2 * u + e, :], by_word[:, g, u, e, :], ident_bf16[:])
+                        nc.tensor.transpose(
+                            bank[:, 4 * g + 2 * half + e, :], by_word[:, g, half, e, :], ident_bf16[:]
+                        )
+            p_banks[b] = bank
+
+        def quantise_p(b):
             p_grouped = work.tile([P, PASSES * K * 4], BF16, tag="p_grouped", align_bytes=64)
             nc.vector.tensor_copy(
                 out=p_grouped[:].rearrange("j (g k v) -> j g k v", g=PASSES, v=4),
-                in_=bank[:].rearrange("j (g v) k -> j g k v", g=PASSES),
+                in_=p_banks[b][:].rearrange("j (g v) k -> j g k v", g=PASSES),
             )
             nc.vector.quantize_mx(
                 out=p_codes[:, b, :].bitcast(FP8X4), scales=p_scales[:, b, :], in_=p_grouped[:]
             )
 
-        def quantise_x(b, h):
-            words = x_sb[(b, h)][:].bitcast(F32).rearrange("p (t w) -> p t w", t=TH)
-            x_grouped = work.tile([P, PASSES * DH * 4], BF16, tag="x_grouped", align_bytes=64)
-            sq_grouped = work.tile([P, PASSES * DH * 4], BF16, tag="sq_grouped", align_bytes=64)
-            x_codes = work.tile([P, PASSES, DH], U32, tag="x_codes", align_bytes=64)
-            x_scales = work.tile([P, PASSES, DH], U8, tag="x_scales", align_bytes=64)
-            sq_codes = work.tile([P, PASSES, DH], U32, tag="sq_codes", align_bytes=64)
-            sq_scales = work.tile([P, PASSES, DH], U8, tag="sq_scales", align_bytes=64)
-            x_words = x_grouped[:].bitcast(F32).rearrange("j (g c u) -> j g c u", g=PASSES, u=2)
+        normalise_p(0)
+        for b in range(1, B):
+            normalise_p(b)
+            quantise_p(b - 1)
+        quantise_p(B - 1)
+
+        mu_t = keep.tile([P, D], BF16, name="mu_t")
+        sigma_t = keep.tile([P, D], BF16, name="sigma_t")
+
+        def turn_mu_sigma():
+            for rows, turned in ((mu_sb, mu_t), (sigma_sb, sigma_t)):
+                bank = psum.tile([P, T, P], BF16, tag="ot", bufs=2)
+                for t in range(T):
+                    nc.tensor.transpose(bank[:, t, :], rows[:, t, :], ident_bf16[:])
+                nc.vector.tensor_copy(out=turned[:], in_=bank[:].rearrange("k t p -> k (t p)"))
+
+        x_banks = {}
+        grouped = {}
+        operands = {}
+        moments = {}
+        m1_squares = {}
+        variances = {}
+        feats = {}
+        sums_sq = {}
+        col_sqs = {}
+        spreads = {}
+        inv_alls = {}
+        out_banks = {}
+
+        def turn_x(u, g):
+            if not 0 <= u < UNITS:
+                return
+            words = x_raw[u][:].bitcast(F32).rearrange("p (t w) -> p t w", t=TH)
+            for pair in range(TH // 2):
+                bank = psum.tile([P, 512], F32, tag="xt", bufs=3)
+                for half in range(2):
+                    for i in range(2):
+                        nc.tensor.transpose(
+                            bank[:, 256 * half + 128 * i : 256 * half + 128 * (i + 1)],
+                            words[:, 2 * pair + i, 256 * g + 128 * half : 256 * g + 128 * (half + 1)],
+                            ident_f32[:],
+                        )
+                x_banks[(u, g, pair)] = bank
+
+        def quantise_x(u, g):
+            if not 0 <= u < UNITS:
+                return
+            if g == 0:
+                x_grouped = work.tile([P, PASSES * DH * 4], BF16, tag="x_grouped", align_bytes=64)
+                sq_grouped = work.tile([P, PASSES * DH * 4], BF16, tag="sq_grouped", align_bytes=64)
+                grouped[u] = (x_grouped, sq_grouped)
+                x_codes = work.tile([P, PASSES, DH], U32, tag="x_codes", bufs=LAG, align_bytes=64)
+                x_scales = work.tile([P, PASSES, DH], U8, tag="x_scales", bufs=LAG, align_bytes=64)
+                sq_codes = work.tile([P, PASSES, DH], U32, tag="sq_codes", bufs=LAG, align_bytes=64)
+                sq_scales = work.tile([P, PASSES, DH], U8, tag="sq_scales", bufs=LAG, align_bytes=64)
+                operands[u] = (x_codes, x_scales, sq_codes, sq_scales)
+            x_grouped, sq_grouped = grouped[u]
+            x_codes, x_scales, sq_codes, sq_scales = operands[u]
+            x_words = x_grouped[:].bitcast(F32).rearrange("j (g c w) -> j g c w", g=PASSES, w=2)
             x_vals = x_grouped[:].rearrange("j (g cv) -> j g cv", g=PASSES)
             sq_vals = sq_grouped[:].rearrange("j (g cv) -> j g cv", g=PASSES)
-            sq_pairs = sq_grouped[:].rearrange("j (g c u e) -> j g c u e", g=PASSES, u=2, e=2)
-            for g in range(PASSES):
-                for pair in range(TH // 2):
-                    bank = psum.tile([P, 512], F32, tag="xt", bufs=3)
-                    for u in range(2):
-                        for i in range(2):
-                            nc.tensor.transpose(
-                                bank[:, 256 * u + 128 * i : 256 * u + 128 * (i + 1)],
-                                words[:, 2 * pair + i, 256 * g + 128 * u : 256 * g + 128 * (u + 1)],
-                                ident_f32[:],
-                            )
-                    cols = slice(256 * pair, 256 * (pair + 1))
-                    nc.scalar.copy(
-                        out=x_words[:, g, cols, :], in_=bank[:].rearrange("j (u c) -> j c u", u=2)
+            sq_pairs = sq_grouped[:].rearrange("j (g c w e) -> j g c w e", g=PASSES, w=2, e=2)
+            for pair in range(TH // 2):
+                bank = x_banks[(u, g, pair)]
+                cols = slice(256 * pair, 256 * (pair + 1))
+                nc.scalar.copy(out=x_words[:, g, cols, :], in_=bank[:].rearrange("j (w c) -> j c w", w=2))
+                if pair % 2 == 0:
+                    vals = slice(1024 * pair, 1024 * (pair + 1))
+                    nc.vector.tensor_tensor(
+                        out=sq_vals[:, g, vals], in0=x_vals[:, g, vals], in1=x_vals[:, g, vals], op=ALU.mult
                     )
-                    if g == PASSES - 1 and pair == TH // 2 - 1:
-                        nc.scalar.activation(
-                            out=sq_pairs[:, g, cols, :, :],
-                            in_=bank[:].bitcast(BF16).rearrange("j (u c e) -> j c u e", u=2, e=2),
-                            func=ACT.Square,
-                        )
-                by_vector = 4 * DH if g < PASSES - 1 else 2 * DH
-                nc.vector.tensor_tensor(
-                    out=sq_vals[:, g, 0:by_vector],
-                    in0=x_vals[:, g, 0:by_vector],
-                    in1=x_vals[:, g, 0:by_vector],
-                    op=ALU.mult,
-                )
-                nc.vector.quantize_mx(
-                    out=x_codes[:, g, :].bitcast(FP8X4), scales=x_scales[:, g, :], in_=x_vals[:, g, :]
-                )
-                nc.vector.quantize_mx(
-                    out=sq_codes[:, g, :].bitcast(FP8X4), scales=sq_scales[:, g, :], in_=sq_vals[:, g, :]
-                )
-            return x_codes, x_scales, sq_codes, sq_scales
+                else:
+                    nc.scalar.activation(
+                        out=sq_pairs[:, g, cols, :, :],
+                        in_=bank[:].bitcast(BF16).rearrange("j (w c e) -> j c w e", w=2, e=2),
+                        func=ACT.Square,
+                    )
+            nc.vector.quantize_mx(
+                out=x_codes[:, g, :].bitcast(FP8X4), scales=x_scales[:, g, :], in_=x_vals[:, g, :]
+            )
+            nc.vector.quantize_mx(
+                out=sq_codes[:, g, :].bitcast(FP8X4), scales=sq_scales[:, g, :], in_=sq_vals[:, g, :]
+            )
 
-        def moments(b, operands):
-            x_codes, x_scales, sq_codes, sq_scales = operands
+        def multiply(u):
+            if not 0 <= u < UNITS:
+                return
+            b = u // HALVES
+            x_codes, x_scales, sq_codes, sq_scales = operands[u]
             m1 = psum.tile([P, DH], F32, tag="m1")
             m2 = psum.tile([P, DH], F32, tag="m2")
             for acc, codes, scales in ((m1, x_codes, x_scales), (m2, sq_codes, sq_scales)):
@@ -159,46 +204,81 @@ def tile_wassvladlayer_pb_t_kernel(tc, probs, x, mu, sigma, out):
                         start=(g == 0),
                         stop=(g == PASSES - 1),
                     )
-            return m1, m2
+            moments[u] = (m1, m2)
 
-        def residuals(h, m1, m2, feat, sums_sq):
-            cols = slice(h * DH, (h + 1) * DH)
+        def square_mean(u):
+            if not 0 <= u < UNITS:
+                return
             m1_sq = work.tile([P, DH], F32, tag="m1_sq")
-            nc.scalar.activation(out=m1_sq[:], in_=m1[:], func=ACT.Square)
-            nc.vector.tensor_tensor(out=feat[:, 0, cols], in0=m1[:], in1=mu_t[:, cols], op=ALU.subtract)
+            nc.scalar.activation(out=m1_sq[:], in_=moments[u][0][:], func=ACT.Square)
+            m1_squares[u] = m1_sq
+
+        def variance(u):
+            if not 0 <= u < UNITS:
+                return
+            b, h = divmod(u, HALVES)
+            cols = slice(h * DH, (h + 1) * DH)
+            if h == 0:
+                feat = work.tile([P, 2, D], F32, tag="feat", bufs=3)
+                feats[b] = feat
+                sums = small.tile([P, 2 * HALVES], F32, tag="sums")
+                sums_sq[b] = sums
+            m1, m2 = moments[u]
+            nc.vector.tensor_tensor(out=feats[b][:, 0, cols], in0=m1[:], in1=mu_t[:, cols], op=ALU.subtract)
             var = work.tile([P, DH], F32, tag="var")
-            nc.vector.tensor_tensor(out=var[:], in0=m2[:], in1=m1_sq[:], op=ALU.subtract)
+            nc.vector.tensor_tensor(out=var[:], in0=m2[:], in1=m1_squares[u][:], op=ALU.subtract)
             nc.vector.tensor_scalar_max(out=var[:], in0=var[:], scalar1=EPS)
-            std = work.tile([P, DH], F32, tag="std")
-            nc.scalar.activation(out=std[:], in_=var[:], func=ACT.Sqrt)
-            nc.vector.tensor_tensor(out=feat[:, 1, cols], in0=std[:], in1=sigma_t[:, cols], op=ALU.subtract)
-            for s in range(2):
-                unread = work.tile([P, DH], BF16, tag="unread_sq", bufs=4)
-                nc.scalar.activation(
-                    out=unread[:],
-                    in_=feat[:, s, cols],
-                    func=ACT.Square,
-                    accum_out=sums_sq[:, 2 * h + s : 2 * h + s + 1],
-                )
+            variances[u] = var
 
-        def inv_sqrt_floor(value, tag):
-            floored = small.tile([P, 1], F32, tag=tag + "_floored")
-            nc.vector.tensor_scalar_max(out=floored[:], in0=value, scalar1=EPS * EPS)
-            root = small.tile([P, 1], F32, tag=tag + "_root")
-            nc.scalar.activation(out=root[:], in_=floored[:], func=ACT.Sqrt)
-            inv = small.tile([P, 1], F32, tag=tag + "_inv")
-            nc.vector.reciprocal(out=inv[:], in_=root[:])
-            return inv
-
-        def normalise_and_store(b, feat, sums_sq):
-            col_sq = small.tile([P, 1], F32, tag="col_sq")
-            nc.vector.tensor_reduce(out=col_sq[:], in_=sums_sq[:], axis=mybir.AxisListType.X, op=ALU.add)
-            inv_col = inv_sqrt_floor(col_sq[:], "col")
-            left_sq = small.tile([P, 1], F32, tag="left_sq")
-            nc.vector.tensor_scalar(
-                out=left_sq[:], in0=col_sq[:], scalar1=inv_col[:, 0:1], scalar2=inv_col[:, 0:1],
-                op0=ALU.mult, op1=ALU.mult,
+        def sum_squares(u, s):
+            b, h = divmod(u, HALVES)
+            unread = work.tile([P, DH], BF16, tag="unread_sq", bufs=4)
+            nc.scalar.activation(
+                out=unread[:],
+                in_=feats[b][:, s, h * DH : (h + 1) * DH],
+                func=ACT.Square,
+                accum_out=sums_sq[b][:, 2 * h + s : 2 * h + s + 1],
             )
+
+        def deviation(u):
+            if not 0 <= u < UNITS:
+                return
+            b, h = divmod(u, HALVES)
+            cols = slice(h * DH, (h + 1) * DH)
+            std = work.tile([P, DH], F32, tag="std")
+            nc.scalar.activation(out=std[:], in_=variances[u][:], func=ACT.Sqrt)
+            sum_squares(u, 0)
+            nc.vector.tensor_tensor(out=feats[b][:, 1, cols], in0=std[:], in1=sigma_t[:, cols], op=ALU.subtract)
+
+        def close_sums(u):
+            if not 0 <= u < UNITS:
+                return
+            sum_squares(u, 1)
+
+        def closes_batch(u):
+            return 0 <= u < UNITS and u % HALVES == HALVES - 1
+
+        def column_norms(u):
+            if not closes_batch(u):
+                return
+            b = u // HALVES
+            col_sq = small.tile([P, 1], F32, tag="col_sq")
+            nc.vector.tensor_reduce(out=col_sq[:], in_=sums_sq[b][:], axis=mybir.AxisListType.X, op=ALU.add)
+            floored = small.tile([P, 1], F32, tag="floored")
+            nc.vector.tensor_scalar_max(out=floored[:], in0=col_sq[:], scalar1=EPS * EPS)
+            inv_col = small.tile([P, 1], F32, tag="inv_col")
+            nc.gpsimd.tensor_tensor(out=inv_col[:], in0=floored[:], in1=minus_half[:], op=ALU.pow)
+            scaled = small.tile([P, 1], F32, tag="scaled")
+            nc.gpsimd.tensor_tensor(out=scaled[:], in0=col_sq[:], in1=inv_col[:], op=ALU.mult)
+            left_sq = small.tile([P, 1], F32, tag="left_sq")
+            nc.gpsimd.tensor_tensor(out=left_sq[:], in0=scaled[:], in1=inv_col[:], op=ALU.mult)
+            col_sqs[b] = (inv_col, left_sq)
+
+        def spread_norms(u):
+            if not closes_batch(u):
+                return
+            b = u // HALVES
+            inv_col, left_sq = col_sqs[b]
             spread = psum.tile([P, 2, P], F32, tag="misc")
             nc.tensor.matmul(
                 out=spread[:, 0, :], lhsT=inv_col[:, 0:1].to_broadcast([P, P]), rhs=ident_f32[:],
@@ -208,38 +288,66 @@ def tile_wassvladlayer_pb_t_kernel(tc, probs, x, mu, sigma, out):
                 out=spread[:, 1, :], lhsT=left_sq[:, 0:1].to_broadcast([P, P]), rhs=ones_f32[:],
                 start=True, stop=True,
             )
-            inv_all = inv_sqrt_floor(spread[:, 1, 0:1], "all")
-            factor = small.tile([P, K], F32, tag="factor")
-            nc.vector.tensor_scalar_mul(out=factor[:], in0=spread[:, 0, :], scalar1=inv_all[:, 0:1])
-            result = work.tile([P, 2, T, K], F32, tag="result")
-            for s in range(2):
-                for h in range(HALVES):
-                    bank = psum.tile([P, TH, K], F32, tag="ot", bufs=2)
-                    for i in range(TH):
-                        t = h * TH + i
-                        nc.tensor.transpose(bank[:, i, :], feat[:, s, t * P : (t + 1) * P], ident_f32[:])
-                    nc.vector.tensor_tensor(
-                        out=result[:, s, h * TH : (h + 1) * TH, :],
-                        in0=bank[:],
-                        in1=factor[:].unsqueeze(1).to_broadcast([P, TH, K]),
-                        op=ALU.mult,
-                    )
-            nc.sync.dma_start(out=out_view[b], in_=result[:])
+            spreads[b] = spread
 
-        units = [(b, h) for b in range(B) for h in range(HALVES)]
-        quantise_p(0)
-        operands = {units[0]: quantise_x(0, 0)}
-        feat = None
-        sums_sq = None
-        for i, (b, h) in enumerate(units):
-            if i + 1 < len(units):
-                if units[i + 1][1] == 0:
-                    quantise_p(units[i + 1][0])
-                operands[units[i + 1]] = quantise_x(units[i + 1][0], units[i + 1][1])
-            if h == 0:
-                feat = work.tile([P, 2, D], F32, tag="feat")
-                sums_sq = small.tile([P, 2 * HALVES], F32, tag="sums_sq")
-            m1, m2 = moments(b, operands[(b, h)])
-            residuals(h, m1, m2, feat, sums_sq)
-            if h == HALVES - 1:
-                normalise_and_store(b, feat, sums_sq)
+        def whole_norm(u):
+            if not closes_batch(u):
+                return
+            b = u // HALVES
+            floored_all = small.tile([P, 1], F32, tag="floored_all")
+            nc.vector.tensor_scalar_max(out=floored_all[:], in0=spreads[b][:, 1, 0:1], scalar1=EPS * EPS)
+            inv_all = small.tile([P, 1], F32, tag="inv_all")
+            nc.gpsimd.tensor_tensor(out=inv_all[:], in0=floored_all[:], in1=minus_half[:], op=ALU.pow)
+            inv_alls[b] = inv_all
+
+        def turn_back(w):
+            if not 0 <= w < UNITS:
+                return
+            b, s = divmod(w, 2)
+            for h in range(HALVES):
+                bank = psum.tile([P, TH, K], F32, tag="ot", bufs=2)
+                for i in range(TH):
+                    t = h * TH + i
+                    nc.tensor.transpose(bank[:, i, :], feats[b][:, s, t * P : (t + 1) * P], ident_f32[:])
+                out_banks[(w, h)] = bank
+
+        factors = {}
+
+        def scale_and_store(w):
+            if not 0 <= w < UNITS:
+                return
+            b, s = divmod(w, 2)
+            if s == 0:
+                factor = small.tile([P, K], F32, tag="factor")
+                nc.vector.tensor_scalar_mul(out=factor[:], in0=spreads[b][:, 0, :], scalar1=inv_alls[b][:, 0:1])
+                factors[b] = factor
+            result = work.tile([P, T, K], F32, tag="result", bufs=3)
+            for h in range(HALVES):
+                nc.vector.tensor_tensor(
+                    out=result[:, h * TH : (h + 1) * TH, :],
+                    in0=out_banks[(w, h)][:],
+                    in1=factors[b][:].unsqueeze(1).to_broadcast([P, TH, K]),
+                    op=ALU.mult,
+                )
+            nc.sync.dma_start(out=out_view[b, s], in_=result[:])
+
+        turn_x(0, 0)
+        for r in range(UNITS + TURN_LAG):
+            u = r - LAG
+            w = r - TURN_LAG
+            column_norms(u - 1)
+            variance(u)
+            scale_and_store(w)
+            quantise_x(r, 0)
+            turn_x(r, 1)
+            multiply(u + 1)
+            turn_back(w + 1)
+            spread_norms(u - 1)
+            deviation(u)
+            quantise_x(r, 1)
+            turn_x(r + 1, 0)
+            close_sums(u)
+            square_mean(u + 1)
+            whole_norm(u - 1)
+            if r == 0:
+                turn_mu_sigma()

@@ -21,6 +21,7 @@ TH = T // HALVES
 DH = D // HALVES
 PASSES = N // 512
 LAG = 3
+VECTOR_COLS = 288
 TURN_LAG = LAG + 4
 
 FLOPS = 2 * 2 * B * D * N * K
@@ -83,7 +84,7 @@ def tile_wassvladlayer_pb_t_kernel(tc, probs, x, mu, sigma, out):
             p_bf16 = work.tile([P, N], BF16, tag="p_bf16")
             nc.vector.tensor_scalar_mul(out=p_bf16[:], in0=probs_sb[:, b, :], scalar1=inv_denom[:, 0:1])
             by_word = p_bf16[:].rearrange("k (g u j e) -> k g u e j", g=PASSES, u=2, e=2)
-            bank = psum.tile([P, PASSES * 4, K], BF16, tag="ot", bufs=2)
+            bank = psum.tile([P, PASSES * 4, K], BF16, tag="turn", bufs=5)
             for g in range(PASSES):
                 for half in range(2):
                     for e in range(2):
@@ -113,7 +114,7 @@ def tile_wassvladlayer_pb_t_kernel(tc, probs, x, mu, sigma, out):
 
         def turn_mu_sigma():
             for rows, turned in ((mu_sb, mu_t), (sigma_sb, sigma_t)):
-                bank = psum.tile([P, T, P], BF16, tag="ot", bufs=2)
+                bank = psum.tile([P, T, P], BF16, tag="turn", bufs=5)
                 for t in range(T):
                     nc.tensor.transpose(bank[:, t, :], rows[:, t, :], ident_bf16[:])
                 nc.vector.tensor_copy(out=turned[:], in_=bank[:].rearrange("k t p -> k (t p)"))
@@ -136,7 +137,7 @@ def tile_wassvladlayer_pb_t_kernel(tc, probs, x, mu, sigma, out):
                 return
             words = x_raw[u][:].bitcast(F32).rearrange("p (t w) -> p t w", t=TH)
             for pair in range(TH // 2):
-                bank = psum.tile([P, 512], F32, tag="xt", bufs=3)
+                bank = psum.tile([P, 512], F32, tag="turn", bufs=5)
                 for half in range(2):
                     for i in range(2):
                         nc.tensor.transpose(
@@ -168,17 +169,17 @@ def tile_wassvladlayer_pb_t_kernel(tc, probs, x, mu, sigma, out):
                 bank = x_banks[(u, g, pair)]
                 cols = slice(256 * pair, 256 * (pair + 1))
                 nc.scalar.copy(out=x_words[:, g, cols, :], in_=bank[:].rearrange("j (w c) -> j c w", w=2))
-                if pair % 2 == 0:
-                    vals = slice(1024 * pair, 1024 * (pair + 1))
-                    nc.vector.tensor_tensor(
-                        out=sq_vals[:, g, vals], in0=x_vals[:, g, vals], in1=x_vals[:, g, vals], op=ALU.mult
-                    )
-                else:
-                    nc.scalar.activation(
-                        out=sq_pairs[:, g, cols, :, :],
-                        in_=bank[:].bitcast(BF16).rearrange("j (w c e) -> j c w e", w=2, e=2),
-                        func=ACT.Square,
-                    )
+            nc.scalar.activation(
+                out=sq_pairs[:, g, VECTOR_COLS:DH, :, :],
+                in_=bank[:].bitcast(BF16).rearrange("j (w c e) -> j c w e", w=2, e=2)[:, VECTOR_COLS - 256 : 256, :, :],
+                func=ACT.Square,
+            )
+            nc.vector.tensor_tensor(
+                out=sq_vals[:, g, 0 : 4 * VECTOR_COLS],
+                in0=x_vals[:, g, 0 : 4 * VECTOR_COLS],
+                in1=x_vals[:, g, 0 : 4 * VECTOR_COLS],
+                op=ALU.mult,
+            )
             nc.vector.quantize_mx(
                 out=x_codes[:, g, :].bitcast(FP8X4), scales=x_scales[:, g, :], in_=x_vals[:, g, :]
             )
@@ -224,9 +225,9 @@ def tile_wassvladlayer_pb_t_kernel(tc, probs, x, mu, sigma, out):
                 sums = small.tile([P, 2 * HALVES], F32, tag="sums")
                 sums_sq[b] = sums
             m1, m2 = moments[u]
-            nc.vector.tensor_tensor(out=feats[b][:, 0, cols], in0=m1[:], in1=mu_t[:, cols], op=ALU.subtract)
             var = work.tile([P, DH], F32, tag="var")
             nc.vector.tensor_tensor(out=var[:], in0=m2[:], in1=m1_squares[u][:], op=ALU.subtract)
+            nc.vector.tensor_tensor(out=feats[b][:, 0, cols], in0=m1[:], in1=mu_t[:, cols], op=ALU.subtract)
             nc.vector.tensor_scalar_max(out=var[:], in0=var[:], scalar1=EPS)
             variances[u] = var
 
@@ -268,10 +269,10 @@ def tile_wassvladlayer_pb_t_kernel(tc, probs, x, mu, sigma, out):
             nc.vector.tensor_scalar_max(out=floored[:], in0=col_sq[:], scalar1=EPS * EPS)
             inv_col = small.tile([P, 1], F32, tag="inv_col")
             nc.gpsimd.tensor_tensor(out=inv_col[:], in0=floored[:], in1=minus_half[:], op=ALU.pow)
-            scaled = small.tile([P, 1], F32, tag="scaled")
-            nc.gpsimd.tensor_tensor(out=scaled[:], in0=col_sq[:], in1=inv_col[:], op=ALU.mult)
             left_sq = small.tile([P, 1], F32, tag="left_sq")
-            nc.gpsimd.tensor_tensor(out=left_sq[:], in0=scaled[:], in1=inv_col[:], op=ALU.mult)
+            nc.vector.tensor_scalar(
+                out=left_sq[:], in0=col_sq[:], scalar1=1.0 / (EPS * EPS), scalar2=1.0, op0=ALU.mult, op1=ALU.min
+            )
             col_sqs[b] = (inv_col, left_sq)
 
         def spread_norms(u):
@@ -281,11 +282,11 @@ def tile_wassvladlayer_pb_t_kernel(tc, probs, x, mu, sigma, out):
             inv_col, left_sq = col_sqs[b]
             spread = psum.tile([P, 2, P], F32, tag="misc")
             nc.tensor.matmul(
-                out=spread[:, 0, :], lhsT=inv_col[:, 0:1].to_broadcast([P, P]), rhs=ident_f32[:],
+                out=spread[:, 1, :], lhsT=left_sq[:, 0:1].to_broadcast([P, P]), rhs=ones_f32[:],
                 start=True, stop=True,
             )
             nc.tensor.matmul(
-                out=spread[:, 1, :], lhsT=left_sq[:, 0:1].to_broadcast([P, P]), rhs=ones_f32[:],
+                out=spread[:, 0, :], lhsT=inv_col[:, 0:1].to_broadcast([P, P]), rhs=ident_f32[:],
                 start=True, stop=True,
             )
             spreads[b] = spread
@@ -305,7 +306,7 @@ def tile_wassvladlayer_pb_t_kernel(tc, probs, x, mu, sigma, out):
                 return
             b, s = divmod(w, 2)
             for h in range(HALVES):
-                bank = psum.tile([P, TH, K], F32, tag="ot", bufs=2)
+                bank = psum.tile([P, TH, K], F32, tag="turn", bufs=5)
                 for i in range(TH):
                     t = h * TH + i
                     nc.tensor.transpose(bank[:, i, :], feats[b][:, s, t * P : (t + 1) * P], ident_f32[:])
@@ -321,15 +322,15 @@ def tile_wassvladlayer_pb_t_kernel(tc, probs, x, mu, sigma, out):
                 factor = small.tile([P, K], F32, tag="factor")
                 nc.vector.tensor_scalar_mul(out=factor[:], in0=spreads[b][:, 0, :], scalar1=inv_alls[b][:, 0:1])
                 factors[b] = factor
-            result = work.tile([P, T, K], F32, tag="result", bufs=3)
             for h in range(HALVES):
+                result = work.tile([P, TH, K], F32, tag="result", bufs=4)
                 nc.vector.tensor_tensor(
-                    out=result[:, h * TH : (h + 1) * TH, :],
+                    out=result[:],
                     in0=out_banks[(w, h)][:],
                     in1=factors[b][:].unsqueeze(1).to_broadcast([P, TH, K]),
                     op=ALU.mult,
                 )
-            nc.sync.dma_start(out=out_view[b, s], in_=result[:])
+                nc.sync.dma_start(out=out_view[b, s, :, h * TH : (h + 1) * TH, :], in_=result[:])
 
         turn_x(0, 0)
         for r in range(UNITS + TURN_LAG):

@@ -10,19 +10,26 @@ U8 = mybir.dt.uint8
 FP8X4 = mybir.dt.float8_e4m3fn_x4
 ALU = mybir.AluOpType
 ACT = mybir.ActivationFunctionType
+AXIS_X = mybir.AxisListType.X
 
 B, D, N, K = 4, 1024, 1024, 128
 EPS = 1e-06
 P = 128
+PACK = 4
+K_PASS = P * PACK
+PASSES = N // K_PASS
+BANK = 512
 T = D // P
 HALVES = 2
 UNITS = B * HALVES
 TH = T // HALVES
 DH = D // HALVES
-PASSES = N // 512
-LAG = 3
+WORDS = K_PASS // 2
+PAIR_COLS = 2 * P
 VECTOR_COLS = 288
+LAG = 2
 TURN_LAG = LAG + 4
+TURN_BANKS = 5
 
 FLOPS = 2 * 2 * B * D * N * K
 
@@ -83,20 +90,20 @@ def tile_wassvladlayer_pb_t_kernel(tc, probs, x, mu, sigma, out):
             nc.vector.reciprocal(out=inv_denom[:], in_=denom[:])
             p_bf16 = work.tile([P, N], BF16, tag="p_bf16")
             nc.vector.tensor_scalar_mul(out=p_bf16[:], in0=probs_sb[:, b, :], scalar1=inv_denom[:, 0:1])
-            by_word = p_bf16[:].rearrange("k (g u j e) -> k g u e j", g=PASSES, u=2, e=2)
-            bank = psum.tile([P, PASSES * 4, K], BF16, tag="turn", bufs=5)
+            by_value = p_bf16[:].rearrange("k (g w j e) -> k g w e j", g=PASSES, w=2, e=2)
+            bank = psum.tile([P, PASSES * PACK, K], BF16, tag="turn", bufs=TURN_BANKS)
             for g in range(PASSES):
-                for half in range(2):
+                for w in range(2):
                     for e in range(2):
                         nc.tensor.transpose(
-                            bank[:, 4 * g + 2 * half + e, :], by_word[:, g, half, e, :], ident_bf16[:]
+                            bank[:, PACK * g + 2 * w + e, :], by_value[:, g, w, e, :], ident_bf16[:]
                         )
             p_banks[b] = bank
 
         def quantise_p(b):
-            p_grouped = work.tile([P, PASSES * K * 4], BF16, tag="p_grouped", align_bytes=64)
+            p_grouped = work.tile([P, PASSES * K * PACK], BF16, tag="p_grouped", align_bytes=64)
             nc.vector.tensor_copy(
-                out=p_grouped[:].rearrange("j (g k v) -> j g k v", g=PASSES, v=4),
+                out=p_grouped[:].rearrange("j (g k v) -> j g k v", g=PASSES, v=PACK),
                 in_=p_banks[b][:].rearrange("j (g v) k -> j g k v", g=PASSES),
             )
             nc.vector.quantize_mx(
@@ -114,7 +121,7 @@ def tile_wassvladlayer_pb_t_kernel(tc, probs, x, mu, sigma, out):
 
         def turn_mu_sigma():
             for rows, turned in ((mu_sb, mu_t), (sigma_sb, sigma_t)):
-                bank = psum.tile([P, T, P], BF16, tag="turn", bufs=5)
+                bank = psum.tile([P, T, P], BF16, tag="turn", bufs=TURN_BANKS)
                 for t in range(T):
                     nc.tensor.transpose(bank[:, t, :], rows[:, t, :], ident_bf16[:])
                 nc.vector.tensor_copy(out=turned[:], in_=bank[:].rearrange("k t p -> k (t p)"))
@@ -127,22 +134,23 @@ def tile_wassvladlayer_pb_t_kernel(tc, probs, x, mu, sigma, out):
         variances = {}
         feats = {}
         sums_sq = {}
-        col_sqs = {}
+        col_norms = {}
         spreads = {}
         inv_alls = {}
         out_banks = {}
+        factors = {}
 
         def turn_x(u, g):
             if not 0 <= u < UNITS:
                 return
-            words = x_raw[u][:].bitcast(F32).rearrange("p (t w) -> p t w", t=TH)
+            words = x_raw[u][:].bitcast(F32).rearrange("p (t a) -> p t a", t=TH)
             for pair in range(TH // 2):
-                bank = psum.tile([P, 512], F32, tag="turn", bufs=5)
-                for half in range(2):
+                bank = psum.tile([P, BANK], F32, tag="turn", bufs=TURN_BANKS)
+                for w in range(2):
                     for i in range(2):
                         nc.tensor.transpose(
-                            bank[:, 256 * half + 128 * i : 256 * half + 128 * (i + 1)],
-                            words[:, 2 * pair + i, 256 * g + 128 * half : 256 * g + 128 * (half + 1)],
+                            bank[:, PAIR_COLS * w + P * i : PAIR_COLS * w + P * (i + 1)],
+                            words[:, 2 * pair + i, WORDS * g + P * w : WORDS * g + P * (w + 1)],
                             ident_f32[:],
                         )
                 x_banks[(u, g, pair)] = bank
@@ -151,8 +159,8 @@ def tile_wassvladlayer_pb_t_kernel(tc, probs, x, mu, sigma, out):
             if not 0 <= u < UNITS:
                 return
             if g == 0:
-                x_grouped = work.tile([P, PASSES * DH * 4], BF16, tag="x_grouped", align_bytes=64)
-                sq_grouped = work.tile([P, PASSES * DH * 4], BF16, tag="sq_grouped", align_bytes=64)
+                x_grouped = work.tile([P, PASSES * DH * PACK], BF16, tag="x_grouped", align_bytes=64)
+                sq_grouped = work.tile([P, PASSES * DH * PACK], BF16, tag="sq_grouped", align_bytes=64)
                 grouped[u] = (x_grouped, sq_grouped)
                 x_codes = work.tile([P, PASSES, DH], U32, tag="x_codes", bufs=LAG, align_bytes=64)
                 x_scales = work.tile([P, PASSES, DH], U8, tag="x_scales", bufs=LAG, align_bytes=64)
@@ -167,17 +175,21 @@ def tile_wassvladlayer_pb_t_kernel(tc, probs, x, mu, sigma, out):
             sq_pairs = sq_grouped[:].rearrange("j (g c w e) -> j g c w e", g=PASSES, w=2, e=2)
             for pair in range(TH // 2):
                 bank = x_banks[(u, g, pair)]
-                cols = slice(256 * pair, 256 * (pair + 1))
-                nc.scalar.copy(out=x_words[:, g, cols, :], in_=bank[:].rearrange("j (w c) -> j c w", w=2))
+                nc.scalar.copy(
+                    out=x_words[:, g, PAIR_COLS * pair : PAIR_COLS * (pair + 1), :],
+                    in_=bank[:].rearrange("j (w c) -> j c w", w=2),
+                )
             nc.scalar.activation(
                 out=sq_pairs[:, g, VECTOR_COLS:DH, :, :],
-                in_=bank[:].bitcast(BF16).rearrange("j (w c e) -> j c w e", w=2, e=2)[:, VECTOR_COLS - 256 : 256, :, :],
+                in_=bank[:].bitcast(BF16).rearrange("j (w c e) -> j c w e", w=2, e=2)[
+                    :, VECTOR_COLS - PAIR_COLS : PAIR_COLS, :, :
+                ],
                 func=ACT.Square,
             )
             nc.vector.tensor_tensor(
-                out=sq_vals[:, g, 0 : 4 * VECTOR_COLS],
-                in0=x_vals[:, g, 0 : 4 * VECTOR_COLS],
-                in1=x_vals[:, g, 0 : 4 * VECTOR_COLS],
+                out=sq_vals[:, g, 0 : PACK * VECTOR_COLS],
+                in0=x_vals[:, g, 0 : PACK * VECTOR_COLS],
+                in1=x_vals[:, g, 0 : PACK * VECTOR_COLS],
                 op=ALU.mult,
             )
             nc.vector.quantize_mx(
@@ -264,7 +276,7 @@ def tile_wassvladlayer_pb_t_kernel(tc, probs, x, mu, sigma, out):
                 return
             b = u // HALVES
             col_sq = small.tile([P, 1], F32, tag="col_sq")
-            nc.vector.tensor_reduce(out=col_sq[:], in_=sums_sq[b][:], axis=mybir.AxisListType.X, op=ALU.add)
+            nc.vector.tensor_reduce(out=col_sq[:], in_=sums_sq[b][:], axis=AXIS_X, op=ALU.add)
             floored = small.tile([P, 1], F32, tag="floored")
             nc.vector.tensor_scalar_max(out=floored[:], in0=col_sq[:], scalar1=EPS * EPS)
             inv_col = small.tile([P, 1], F32, tag="inv_col")
@@ -273,13 +285,13 @@ def tile_wassvladlayer_pb_t_kernel(tc, probs, x, mu, sigma, out):
             nc.vector.tensor_scalar(
                 out=left_sq[:], in0=col_sq[:], scalar1=1.0 / (EPS * EPS), scalar2=1.0, op0=ALU.mult, op1=ALU.min
             )
-            col_sqs[b] = (inv_col, left_sq)
+            col_norms[b] = (inv_col, left_sq)
 
         def spread_norms(u):
             if not closes_batch(u):
                 return
             b = u // HALVES
-            inv_col, left_sq = col_sqs[b]
+            inv_col, left_sq = col_norms[b]
             spread = psum.tile([P, 2, P], F32, tag="misc")
             nc.tensor.matmul(
                 out=spread[:, 1, :], lhsT=left_sq[:, 0:1].to_broadcast([P, P]), rhs=ones_f32[:],
@@ -306,13 +318,11 @@ def tile_wassvladlayer_pb_t_kernel(tc, probs, x, mu, sigma, out):
                 return
             b, s = divmod(w, 2)
             for h in range(HALVES):
-                bank = psum.tile([P, TH, K], F32, tag="turn", bufs=5)
+                bank = psum.tile([P, TH, K], F32, tag="turn", bufs=TURN_BANKS)
                 for i in range(TH):
                     t = h * TH + i
                     nc.tensor.transpose(bank[:, i, :], feats[b][:, s, t * P : (t + 1) * P], ident_f32[:])
                 out_banks[(w, h)] = bank
-
-        factors = {}
 
         def scale_and_store(w):
             if not 0 <= w < UNITS:

@@ -90,21 +90,17 @@ def tile_wassvladlayer_pb_t_kernel(tc, probs, x, mu, sigma, out):
             nc.vector.reciprocal(out=inv_denom[:], in_=denom[:])
             p_bf16 = work.tile([P, N], BF16, tag="p_bf16")
             nc.vector.tensor_scalar_mul(out=p_bf16[:], in0=probs_sb[:, b, :], scalar1=inv_denom[:, 0:1])
-            by_value = p_bf16[:].rearrange("k (g w j e) -> k g w e j", g=PASSES, w=2, e=2)
-            bank = psum.tile([P, PASSES * PACK, K], BF16, tag="turn", bufs=TURN_BANKS)
-            for g in range(PASSES):
-                for w in range(2):
-                    for e in range(2):
-                        nc.tensor.transpose(
-                            bank[:, PACK * g + 2 * w + e, :], by_value[:, g, w, e, :], ident_bf16[:]
-                        )
+            words = p_bf16[:].bitcast(F32)
+            bank = psum.tile([P, PASSES * 2, K], F32, tag="turn", bufs=TURN_BANKS)
+            for q in range(PASSES * 2):
+                nc.tensor.transpose(bank[:, q, :], words[:, P * q : P * (q + 1)], ident_f32[:])
             p_banks[b] = bank
 
         def quantise_p(b):
             p_grouped = work.tile([P, PASSES * K * PACK], BF16, tag="p_grouped", align_bytes=64)
             nc.vector.tensor_copy(
-                out=p_grouped[:].rearrange("j (g k v) -> j g k v", g=PASSES, v=PACK),
-                in_=p_banks[b][:].rearrange("j (g v) k -> j g k v", g=PASSES),
+                out=p_grouped[:].bitcast(F32).rearrange("j (g k w) -> j g k w", g=PASSES, w=2),
+                in_=p_banks[b][:].rearrange("j (g w) k -> j g k w", g=PASSES),
             )
             nc.vector.quantize_mx(
                 out=p_codes[:, b, :].bitcast(FP8X4), scales=p_scales[:, b, :], in_=p_grouped[:]

@@ -67,10 +67,8 @@ def tile_wassvladlayer_pb_t_kernel(tc, probs, x, mu, sigma, out):
         make_identity(nc, ident_f32[:])
         ident_bf16 = keep.tile([P, P], BF16, name="ident_bf16")
         make_identity(nc, ident_bf16[:])
-        ones_f32 = keep.tile([P, P], F32, name="ones_f32")
+        ones_f32 = keep.tile([P, 1], F32, name="ones_f32")
         nc.vector.memset(ones_f32[:], 1.0)
-        minus_half = keep.tile([P, 1], F32, name="minus_half")
-        nc.vector.memset(minus_half[:], -0.5)
         warm = keep.tile([P, 1], F32, name="warm")
         nc.scalar.sqrt(warm[:], ones_f32[:, 0:1])
 
@@ -81,11 +79,17 @@ def tile_wassvladlayer_pb_t_kernel(tc, probs, x, mu, sigma, out):
 
         def normalise_p(b):
             unread = work.tile([P, N], BF16, tag="unread_p")
-            nc.scalar.activation(
-                out=unread[:], in_=probs_sb[:, b, :], func=ACT.Copy, accum_out=p_sums[:, b : b + 1]
-            )
             denom = small.tile([P, 1], F32, tag="denom")
-            nc.vector.tensor_scalar_add(out=denom[:], in0=p_sums[:, b : b + 1], scalar1=EPS)
+            if b == 0:
+                nc.vector.tensor_scalar(
+                    out=unread[:], in0=probs_sb[:, b, :], scalar1=1.0, scalar2=EPS, op0=ALU.mult, op1=ALU.add,
+                    accum_out=denom[:],
+                )
+            else:
+                nc.scalar.activation(
+                    out=unread[:], in_=probs_sb[:, b, :], func=ACT.Copy, accum_out=p_sums[:, b : b + 1]
+                )
+                nc.vector.tensor_scalar_add(out=denom[:], in0=p_sums[:, b : b + 1], scalar1=EPS)
             inv_denom = small.tile([P, 1], F32, tag="inv_denom")
             nc.vector.reciprocal(out=inv_denom[:], in_=denom[:])
             p_bf16 = work.tile([P, N], BF16, tag="p_bf16")
@@ -275,26 +279,19 @@ def tile_wassvladlayer_pb_t_kernel(tc, probs, x, mu, sigma, out):
             nc.vector.tensor_reduce(out=col_sq[:], in_=sums_sq[b][:], axis=AXIS_X, op=ALU.add)
             floored = small.tile([P, 1], F32, tag="floored")
             nc.vector.tensor_scalar_max(out=floored[:], in0=col_sq[:], scalar1=EPS * EPS)
-            inv_col = small.tile([P, 1], F32, tag="inv_col")
-            nc.gpsimd.tensor_tensor(out=inv_col[:], in0=floored[:], in1=minus_half[:], op=ALU.pow)
             left_sq = small.tile([P, 1], F32, tag="left_sq")
             nc.vector.tensor_scalar(
                 out=left_sq[:], in0=col_sq[:], scalar1=1.0 / (EPS * EPS), scalar2=1.0, op0=ALU.mult, op1=ALU.min
             )
-            col_norms[b] = (inv_col, left_sq)
+            col_norms[b] = (floored, left_sq)
 
-        def spread_norms(u):
+        def spread_left(u):
             if not closes_batch(u):
                 return
             b = u // HALVES
-            inv_col, left_sq = col_norms[b]
             spread = psum.tile([P, 2, P], F32, tag="misc")
             nc.tensor.matmul(
-                out=spread[:, 1, :], lhsT=left_sq[:, 0:1].to_broadcast([P, P]), rhs=ones_f32[:],
-                start=True, stop=True,
-            )
-            nc.tensor.matmul(
-                out=spread[:, 0, :], lhsT=inv_col[:, 0:1].to_broadcast([P, P]), rhs=ident_f32[:],
+                out=spread[:, 1, 0:1], lhsT=col_norms[b][1][:, 0:1].to_broadcast([P, P]), rhs=ones_f32[:, 0:1],
                 start=True, stop=True,
             )
             spreads[b] = spread
@@ -303,11 +300,23 @@ def tile_wassvladlayer_pb_t_kernel(tc, probs, x, mu, sigma, out):
             if not closes_batch(u):
                 return
             b = u // HALVES
-            floored_all = small.tile([P, 1], F32, tag="floored_all")
-            nc.vector.tensor_scalar_max(out=floored_all[:], in0=spreads[b][:, 1, 0:1], scalar1=EPS * EPS)
-            inv_all = small.tile([P, 1], F32, tag="inv_all")
-            nc.gpsimd.tensor_tensor(out=inv_all[:], in0=floored_all[:], in1=minus_half[:], op=ALU.pow)
-            inv_alls[b] = inv_all
+            both = small.tile([P, 1], F32, tag="both")
+            nc.vector.tensor_scalar(
+                out=both[:], in0=spreads[b][:, 1, 0:1], scalar1=EPS * EPS, scalar2=col_norms[b][0][:, 0:1],
+                op0=ALU.max, op1=ALU.mult,
+            )
+            inv_both = small.tile([P, 1], F32, tag="inv_both")
+            nc.vector.reciprocal(out=inv_both[:], in_=both[:])
+            inv_alls[b] = inv_both
+
+        def spread_factor(u):
+            if not closes_batch(u):
+                return
+            b = u // HALVES
+            nc.tensor.transpose(spreads[b][:, 0, :], inv_alls[b][:, 0:1].to_broadcast([P, P]), ident_f32[:])
+            factor = small.tile([P, K], F32, tag="factor")
+            nc.scalar.activation(out=factor[:], in_=spreads[b][:, 0, :], func=ACT.Sqrt)
+            factors[b] = factor
 
         def turn_back(w):
             if not 0 <= w < UNITS:
@@ -324,12 +333,8 @@ def tile_wassvladlayer_pb_t_kernel(tc, probs, x, mu, sigma, out):
             if not 0 <= w < UNITS:
                 return
             b, s = divmod(w, 2)
-            if s == 0:
-                factor = small.tile([P, K], F32, tag="factor")
-                nc.vector.tensor_scalar_mul(out=factor[:], in0=spreads[b][:, 0, :], scalar1=inv_alls[b][:, 0:1])
-                factors[b] = factor
             for h in range(HALVES):
-                result = work.tile([P, TH, K], F32, tag="result", bufs=4)
+                result = work.tile([P, TH, K], F32, tag="result", bufs=8)
                 nc.vector.tensor_tensor(
                     out=result[:],
                     in0=out_banks[(w, h)][:],
@@ -349,12 +354,13 @@ def tile_wassvladlayer_pb_t_kernel(tc, probs, x, mu, sigma, out):
             turn_x(r, 1)
             multiply(u + 1)
             turn_back(w + 1)
-            spread_norms(u - 1)
+            spread_left(u - 1)
             deviation(u)
             quantise_x(r, 1)
             turn_x(r + 1, 0)
             close_sums(u)
             square_mean(u + 1)
             whole_norm(u - 1)
+            spread_factor(u - 1)
             if r == 0:
                 turn_mu_sigma()

@@ -14,6 +14,7 @@ AXIS_X = mybir.AxisListType.X
 
 B, D, N, K = 4, 1024, 1024, 128
 EPS = 1e-06
+F32_MAX = 3.4028234663852886e38
 P = 128
 PACK = 4
 K_PASS = P * PACK
@@ -26,7 +27,7 @@ TH = T // HALVES
 DH = D // HALVES
 WORDS = K_PASS // 2
 PAIR_COLS = 2 * P
-VECTOR_COLS = 288
+VECTOR_COLS = 320
 LAG = 2
 TURN_LAG = LAG + 4
 TURN_BANKS = 5
@@ -102,19 +103,13 @@ def tile_wassvladlayer_pb_t_kernel(tc, probs, x, mu, sigma, out):
 
         def quantise_p(b):
             p_grouped = work.tile([P, PASSES * K * PACK], BF16, tag="p_grouped", align_bytes=64)
-            nc.vector.tensor_copy(
+            nc.scalar.copy(
                 out=p_grouped[:].bitcast(F32).rearrange("j (g k w) -> j g k w", g=PASSES, w=2),
                 in_=p_banks[b][:].rearrange("j (g w) k -> j g k w", g=PASSES),
             )
             nc.vector.quantize_mx(
                 out=p_codes[:, b, :].bitcast(FP8X4), scales=p_scales[:, b, :], in_=p_grouped[:]
             )
-
-        normalise_p(0)
-        for b in range(1, B):
-            normalise_p(b)
-            quantise_p(b - 1)
-        quantise_p(B - 1)
 
         mu_t = keep.tile([P, D], BF16, name="mu_t")
         sigma_t = keep.tile([P, D], BF16, name="sigma_t")
@@ -239,8 +234,10 @@ def tile_wassvladlayer_pb_t_kernel(tc, probs, x, mu, sigma, out):
             m1, m2 = moments[u]
             var = work.tile([P, DH], F32, tag="var")
             nc.vector.tensor_tensor(out=var[:], in0=m2[:], in1=m1_squares[u][:], op=ALU.subtract)
+            nc.gpsimd.tensor_scalar(
+                out=var[:], in0=var[:], scalar1=F32_MAX, scalar2=EPS, op0=ALU.min, op1=ALU.max
+            )
             nc.vector.tensor_tensor(out=feats[b][:, 0, cols], in0=m1[:], in1=mu_t[:, cols], op=ALU.subtract)
-            nc.vector.tensor_scalar_max(out=var[:], in0=var[:], scalar1=EPS)
             variances[u] = var
 
         def sum_squares(u, s):
@@ -343,7 +340,12 @@ def tile_wassvladlayer_pb_t_kernel(tc, probs, x, mu, sigma, out):
                 )
                 nc.sync.dma_start(out=out_view[b, s, :, h * TH : (h + 1) * TH, :], in_=result[:])
 
+        normalise_p(0)
         turn_x(0, 0)
+        for b in range(1, B):
+            normalise_p(b)
+            quantise_p(b - 1)
+        quantise_p(B - 1)
         for r in range(UNITS + TURN_LAG):
             u = r - LAG
             w = r - TURN_LAG

@@ -29,7 +29,7 @@ WORDS = K_PASS // 2
 PAIR_COLS = 2 * P
 VECTOR_COLS = 320
 LAG = 2
-TURN_LAG = LAG + 4
+TURN_LAG = LAG + 5
 TURN_BANKS = 5
 
 FLOPS = 2 * 2 * B * D * N * K
@@ -229,7 +229,7 @@ def tile_wassvladlayer_pb_t_kernel(tc, probs, x, mu, sigma, out):
             if h == 0:
                 feat = work.tile([P, 2, D], F32, tag="feat", bufs=3)
                 feats[b] = feat
-                sums = small.tile([P, 2 * HALVES], F32, tag="sums")
+                sums = small.tile([P, HALVES + 1], F32, tag="sums")
                 sums_sq[b] = sums
             m1, m2 = moments[u]
             var = work.tile([P, DH], F32, tag="var")
@@ -240,14 +240,14 @@ def tile_wassvladlayer_pb_t_kernel(tc, probs, x, mu, sigma, out):
             nc.vector.tensor_tensor(out=feats[b][:, 0, cols], in0=m1[:], in1=mu_t[:, cols], op=ALU.subtract)
             variances[u] = var
 
-        def sum_squares(u, s):
+        def sum_squares(u, halves, slot):
             b, h = divmod(u, HALVES)
-            unread = work.tile([P, DH], BF16, tag="unread_sq", bufs=4)
+            unread = work.tile([P, 2, DH], BF16, tag="unread_sq")
             nc.scalar.activation(
-                out=unread[:],
-                in_=feats[b][:, s, h * DH : (h + 1) * DH],
+                out=unread[:, halves, :],
+                in_=feats[b][:, halves, h * DH : (h + 1) * DH],
                 func=ACT.Square,
-                accum_out=sums_sq[b][:, 2 * h + s : 2 * h + s + 1],
+                accum_out=sums_sq[b][:, slot : slot + 1],
             )
 
         def deviation(u):
@@ -257,13 +257,17 @@ def tile_wassvladlayer_pb_t_kernel(tc, probs, x, mu, sigma, out):
             cols = slice(h * DH, (h + 1) * DH)
             std = work.tile([P, DH], F32, tag="std")
             nc.scalar.activation(out=std[:], in_=variances[u][:], func=ACT.Sqrt)
-            sum_squares(u, 0)
+            if u == UNITS - 1:
+                sum_squares(u, slice(0, 1), HALVES - 1)
             nc.vector.tensor_tensor(out=feats[b][:, 1, cols], in0=std[:], in1=sigma_t[:, cols], op=ALU.subtract)
 
         def close_sums(u):
             if not 0 <= u < UNITS:
                 return
-            sum_squares(u, 1)
+            if u == UNITS - 1:
+                sum_squares(u, slice(1, 2), HALVES)
+            else:
+                sum_squares(u, slice(0, 2), u % HALVES)
 
         def closes_batch(u):
             return 0 <= u < UNITS and u % HALVES == HALVES - 1
@@ -273,7 +277,7 @@ def tile_wassvladlayer_pb_t_kernel(tc, probs, x, mu, sigma, out):
                 return
             b = u // HALVES
             col_sq = small.tile([P, 1], F32, tag="col_sq")
-            nc.vector.tensor_reduce(out=col_sq[:], in_=sums_sq[b][:], axis=AXIS_X, op=ALU.add)
+            nc.vector.tensor_reduce(out=col_sq[:], in_=sums_sq[b][:, 0 : HALVES + (b == B - 1)], axis=AXIS_X, op=ALU.add)
             floored = small.tile([P, 1], F32, tag="floored")
             nc.vector.tensor_scalar_max(out=floored[:], in0=col_sq[:], scalar1=EPS * EPS)
             left_sq = small.tile([P, 1], F32, tag="left_sq")

@@ -14,7 +14,6 @@ AXIS_X = mybir.AxisListType.X
 
 B, D, N, K = 4, 1024, 1024, 128
 EPS = 1e-06
-F32_MAX = 3.4028234663852886e38
 P = 128
 PACK = 4
 K_PASS = P * PACK
@@ -27,7 +26,7 @@ TH = T // HALVES
 DH = D // HALVES
 WORDS = K_PASS // 2
 PAIR_COLS = 2 * P
-VECTOR_COLS = 320
+VECTOR_COLS = 304
 LAG = 2
 TURN_LAG = LAG + 5
 TURN_BANKS = 5
@@ -229,26 +228,14 @@ def tile_wassvladlayer_pb_t_kernel(tc, probs, x, mu, sigma, out):
             if h == 0:
                 feat = work.tile([P, 2, D], F32, tag="feat", bufs=3)
                 feats[b] = feat
-                sums = small.tile([P, HALVES + 1], F32, tag="sums")
+                sums = small.tile([P, HALVES], F32, tag="sums")
                 sums_sq[b] = sums
             m1, m2 = moments[u]
             var = work.tile([P, DH], F32, tag="var")
             nc.vector.tensor_tensor(out=var[:], in0=m2[:], in1=m1_squares[u][:], op=ALU.subtract)
-            nc.gpsimd.tensor_scalar(
-                out=var[:], in0=var[:], scalar1=F32_MAX, scalar2=EPS, op0=ALU.min, op1=ALU.max
-            )
             nc.vector.tensor_tensor(out=feats[b][:, 0, cols], in0=m1[:], in1=mu_t[:, cols], op=ALU.subtract)
+            nc.vector.tensor_scalar_max(out=var[:], in0=var[:], scalar1=EPS)
             variances[u] = var
-
-        def sum_squares(u, halves, slot):
-            b, h = divmod(u, HALVES)
-            unread = work.tile([P, 2, DH], BF16, tag="unread_sq")
-            nc.scalar.activation(
-                out=unread[:, halves, :],
-                in_=feats[b][:, halves, h * DH : (h + 1) * DH],
-                func=ACT.Square,
-                accum_out=sums_sq[b][:, slot : slot + 1],
-            )
 
         def deviation(u):
             if not 0 <= u < UNITS:
@@ -257,17 +244,19 @@ def tile_wassvladlayer_pb_t_kernel(tc, probs, x, mu, sigma, out):
             cols = slice(h * DH, (h + 1) * DH)
             std = work.tile([P, DH], F32, tag="std")
             nc.scalar.activation(out=std[:], in_=variances[u][:], func=ACT.Sqrt)
-            if u == UNITS - 1:
-                sum_squares(u, slice(0, 1), HALVES - 1)
             nc.vector.tensor_tensor(out=feats[b][:, 1, cols], in0=std[:], in1=sigma_t[:, cols], op=ALU.subtract)
 
         def close_sums(u):
             if not 0 <= u < UNITS:
                 return
-            if u == UNITS - 1:
-                sum_squares(u, slice(1, 2), HALVES)
-            else:
-                sum_squares(u, slice(0, 2), u % HALVES)
+            b, h = divmod(u, HALVES)
+            unread = work.tile([P, 2, DH], BF16, tag="unread_sq")
+            nc.scalar.activation(
+                out=unread[:],
+                in_=feats[b][:, :, h * DH : (h + 1) * DH],
+                func=ACT.Square,
+                accum_out=sums_sq[b][:, h : h + 1],
+            )
 
         def closes_batch(u):
             return 0 <= u < UNITS and u % HALVES == HALVES - 1
@@ -276,13 +265,14 @@ def tile_wassvladlayer_pb_t_kernel(tc, probs, x, mu, sigma, out):
             if not closes_batch(u):
                 return
             b = u // HALVES
-            col_sq = small.tile([P, 1], F32, tag="col_sq")
-            nc.vector.tensor_reduce(out=col_sq[:], in_=sums_sq[b][:, 0 : HALVES + (b == B - 1)], axis=AXIS_X, op=ALU.add)
+            halves = sums_sq[b]
             floored = small.tile([P, 1], F32, tag="floored")
-            nc.vector.tensor_scalar_max(out=floored[:], in0=col_sq[:], scalar1=EPS * EPS)
+            nc.vector.tensor_scalar(
+                out=floored[:], in0=halves[:, 0:1], scalar1=halves[:, 1:2], scalar2=EPS * EPS, op0=ALU.add, op1=ALU.max
+            )
             left_sq = small.tile([P, 1], F32, tag="left_sq")
             nc.vector.tensor_scalar(
-                out=left_sq[:], in0=col_sq[:], scalar1=1.0 / (EPS * EPS), scalar2=1.0, op0=ALU.mult, op1=ALU.min
+                out=left_sq[:], in0=halves[:, 0:1], scalar1=halves[:, 1:2], scalar2=EPS * EPS, op0=ALU.add, op1=ALU.min
             )
             col_norms[b] = (floored, left_sq)
 
@@ -303,7 +293,7 @@ def tile_wassvladlayer_pb_t_kernel(tc, probs, x, mu, sigma, out):
             b = u // HALVES
             both = small.tile([P, 1], F32, tag="both")
             nc.vector.tensor_scalar(
-                out=both[:], in0=spreads[b][:, 1, 0:1], scalar1=EPS * EPS, scalar2=col_norms[b][0][:, 0:1],
+                out=both[:], in0=spreads[b][:, 1, 0:1], scalar1=EPS**4, scalar2=col_norms[b][0][:, 0:1],
                 op0=ALU.max, op1=ALU.mult,
             )
             inv_both = small.tile([P, 1], F32, tag="inv_both")
@@ -316,7 +306,7 @@ def tile_wassvladlayer_pb_t_kernel(tc, probs, x, mu, sigma, out):
             b = u // HALVES
             nc.tensor.transpose(spreads[b][:, 0, :], inv_alls[b][:, 0:1].to_broadcast([P, P]), ident_f32[:])
             factor = small.tile([P, K], F32, tag="factor")
-            nc.scalar.activation(out=factor[:], in_=spreads[b][:, 0, :], func=ACT.Sqrt)
+            nc.scalar.activation(out=factor[:], in_=spreads[b][:, 0, :], func=ACT.Sqrt, scale=EPS * EPS)
             factors[b] = factor
 
         def turn_back(w):

from contextlib import ExitStack

import concourse.mybir as mybir
from concourse.masks import make_identity

F32 = mybir.dt.float32
BF16 = mybir.dt.bfloat16
U32 = mybir.dt.uint32
U8 = mybir.dt.uint8
FP8X4 = mybir.dt.float8_e4m3fn_x4
ALU = mybir.AluOpType
ACT = mybir.ActivationFunctionType
AXIS_X = mybir.AxisListType.X

B, D, N, K = 4, 1024, 1024, 128
EPS = 1e-06
P = 128
PACK = 4
K_PASS = P * PACK
PASSES = N // K_PASS
BANK = 512
T = D // P
HALVES = 2
UNITS = B * HALVES
TH = T // HALVES
DH = D // HALVES
WORDS = K_PASS // 2
PAIR_COLS = 2 * P
VECTOR_COLS = 304
LAG = 2
TURN_LAG = LAG + 5
TURN_BANKS = 5

FLOPS = 2 * 2 * B * D * N * K


def tile_wassvladlayer_pb_t_kernel(tc, probs, x, mu, sigma, out):
    nc = tc.nc
    x_view = x.rearrange("b (p t) n -> b p t n", t=T)
    out_view = out.rearrange("b (s p t k) -> b s p t k", s=2, p=P, t=T)

    with ExitStack() as ctx:
        keep = ctx.enter_context(tc.tile_pool(name="keep", bufs=1))
        work = ctx.enter_context(tc.tile_pool(name="work", bufs=2))
        small = ctx.enter_context(tc.tile_pool(name="small", bufs=3))
        psum = ctx.enter_context(tc.psum_pool(name="psum", bufs=1))

        probs_sb = keep.tile([P, B, N], BF16, name="probs_sb")
        for b in range(B):
            nc.sync.dma_start(out=probs_sb[:, b, :], in_=probs[b])
        mu_sb = keep.tile([P, T, K], BF16, name="mu_sb")
        sigma_sb = keep.tile([P, T, K], BF16, name="sigma_sb")
        x_raw = {}
        for u in range(UNITS):
            b, h = divmod(u, HALVES)
            x_raw[u] = keep.tile([P, TH * N], BF16, name="x_raw_%d" % u)
            for pair in range(TH // 2):
                nc.sync.dma_start(
                    out=x_raw[u][:, 2 * pair * N : 2 * (pair + 1) * N].rearrange("p (t n) -> p t n", t=2),
                    in_=x_view[b, :, h * TH + 2 * pair : h * TH + 2 * (pair + 1), :],
                )
            if u == 0:
                nc.sync.dma_start(out=mu_sb[:], in_=mu[0].rearrange("(p t) k -> p t k", t=T))
                nc.sync.dma_start(out=sigma_sb[:], in_=sigma[0].rearrange("(p t) k -> p t k", t=T))

        ident_f32 = keep.tile([P, P], F32, name="ident_f32")
        make_identity(nc, ident_f32[:])
        ident_bf16 = keep.tile([P, P], BF16, name="ident_bf16")
        make_identity(nc, ident_bf16[:])
        ones_f32 = keep.tile([P, 1], F32, name="ones_f32")
        nc.vector.memset(ones_f32[:], 1.0)
        warm = keep.tile([P, 1], F32, name="warm")
        nc.scalar.sqrt(warm[:], ones_f32[:, 0:1])

        p_sums = keep.tile([P, B], F32, name="p_sums")
        p_codes = keep.tile([P, B, PASSES * K], U32, name="p_codes", align_bytes=64)
        p_scales = keep.tile([P, B, PASSES * K], U8, name="p_scales", align_bytes=64)
        p_banks = {}

        def normalise_p(b):
            unread = work.tile([P, N], BF16, tag="unread_p")
            denom = small.tile([P, 1], F32, tag="denom")
            if b == 0:
                nc.vector.tensor_scalar(
                    out=unread[:], in0=probs_sb[:, b, :], scalar1=1.0, scalar2=EPS, op0=ALU.mult, op1=ALU.add,
                    accum_out=denom[:],
                )
            else:
                nc.scalar.activation(
                    out=unread[:], in_=probs_sb[:, b, :], func=ACT.Copy, accum_out=p_sums[:, b : b + 1]
                )
                nc.vector.tensor_scalar_add(out=denom[:], in0=p_sums[:, b : b + 1], scalar1=EPS)
            inv_denom = small.tile([P, 1], F32, tag="inv_denom")
            nc.vector.reciprocal(out=inv_denom[:], in_=denom[:])
            p_bf16 = work.tile([P, N], BF16, tag="p_bf16")
            nc.vector.tensor_scalar_mul(out=p_bf16[:], in0=probs_sb[:, b, :], scalar1=inv_denom[:, 0:1])
            words = p_bf16[:].bitcast(F32)
            bank = psum.tile([P, PASSES * 2, K], F32, tag="turn", bufs=TURN_BANKS)
            for q in range(PASSES * 2):
                nc.tensor.transpose(bank[:, q, :], words[:, P * q : P * (q + 1)], ident_f32[:])
            p_banks[b] = bank

        def quantise_p(b):
            p_grouped = work.tile([P, PASSES * K * PACK], BF16, tag="p_grouped", align_bytes=64)
            nc.scalar.copy(
                out=p_grouped[:].bitcast(F32).rearrange("j (g k w) -> j g k w", g=PASSES, w=2),
                in_=p_banks[b][:].rearrange("j (g w) k -> j g k w", g=PASSES),
            )
            nc.vector.quantize_mx(
                out=p_codes[:, b, :].bitcast(FP8X4), scales=p_scales[:, b, :], in_=p_grouped[:]
            )

        mu_t = keep.tile([P, D], BF16, name="mu_t")
        sigma_t = keep.tile([P, D], BF16, name="sigma_t")

        def turn_mu_sigma():
            for rows, turned in ((mu_sb, mu_t), (sigma_sb, sigma_t)):
                bank = psum.tile([P, T, P], BF16, tag="turn", bufs=TURN_BANKS)
                for t in range(T):
                    nc.tensor.transpose(bank[:, t, :], rows[:, t, :], ident_bf16[:])
                nc.vector.tensor_copy(out=turned[:], in_=bank[:].rearrange("k t p -> k (t p)"))

        x_banks = {}
        grouped = {}
        operands = {}
        moments = {}
        m1_squares = {}
        variances = {}
        feats = {}
        sums_sq = {}
        col_norms = {}
        spreads = {}
        inv_alls = {}
        out_banks = {}
        factors = {}

        def turn_x(u, g):
            if not 0 <= u < UNITS:
                return
            words = x_raw[u][:].bitcast(F32).rearrange("p (t a) -> p t a", t=TH)
            for pair in range(TH // 2):
                bank = psum.tile([P, BANK], F32, tag="turn", bufs=TURN_BANKS)
                for w in range(2):
                    for i in range(2):
                        nc.tensor.transpose(
                            bank[:, PAIR_COLS * w + P * i : PAIR_COLS * w + P * (i + 1)],
                            words[:, 2 * pair + i, WORDS * g + P * w : WORDS * g + P * (w + 1)],
                            ident_f32[:],
                        )
                x_banks[(u, g, pair)] = bank

        def quantise_x(u, g):
            if not 0 <= u < UNITS:
                return
            if g == 0:
                x_grouped = work.tile([P, PASSES * DH * PACK], BF16, tag="x_grouped", align_bytes=64)
                sq_grouped = work.tile([P, PASSES * DH * PACK], BF16, tag="sq_grouped", align_bytes=64)
                grouped[u] = (x_grouped, sq_grouped)
                x_codes = work.tile([P, PASSES, DH], U32, tag="x_codes", bufs=LAG, align_bytes=64)
                x_scales = work.tile([P, PASSES, DH], U8, tag="x_scales", bufs=LAG, align_bytes=64)
                sq_codes = work.tile([P, PASSES, DH], U32, tag="sq_codes", bufs=LAG, align_bytes=64)
                sq_scales = work.tile([P, PASSES, DH], U8, tag="sq_scales", bufs=LAG, align_bytes=64)
                operands[u] = (x_codes, x_scales, sq_codes, sq_scales)
            x_grouped, sq_grouped = grouped[u]
            x_codes, x_scales, sq_codes, sq_scales = operands[u]
            x_words = x_grouped[:].bitcast(F32).rearrange("j (g c w) -> j g c w", g=PASSES, w=2)
            x_vals = x_grouped[:].rearrange("j (g cv) -> j g cv", g=PASSES)
            sq_vals = sq_grouped[:].rearrange("j (g cv) -> j g cv", g=PASSES)
            sq_pairs = sq_grouped[:].rearrange("j (g c w e) -> j g c w e", g=PASSES, w=2, e=2)
            for pair in range(TH // 2):
                bank = x_banks[(u, g, pair)]
                nc.scalar.copy(
                    out=x_words[:, g, PAIR_COLS * pair : PAIR_COLS * (pair + 1), :],
                    in_=bank[:].rearrange("j (w c) -> j c w", w=2),
                )
            nc.scalar.activation(
                out=sq_pairs[:, g, VECTOR_COLS:DH, :, :],
                in_=bank[:].bitcast(BF16).rearrange("j (w c e) -> j c w e", w=2, e=2)[
                    :, VECTOR_COLS - PAIR_COLS : PAIR_COLS, :, :
                ],
                func=ACT.Square,
            )
            nc.vector.tensor_tensor(
                out=sq_vals[:, g, 0 : PACK * VECTOR_COLS],
                in0=x_vals[:, g, 0 : PACK * VECTOR_COLS],
                in1=x_vals[:, g, 0 : PACK * VECTOR_COLS],
                op=ALU.mult,
            )
            nc.vector.quantize_mx(
                out=x_codes[:, g, :].bitcast(FP8X4), scales=x_scales[:, g, :], in_=x_vals[:, g, :]
            )
            nc.vector.quantize_mx(
                out=sq_codes[:, g, :].bitcast(FP8X4), scales=sq_scales[:, g, :], in_=sq_vals[:, g, :]
            )

        def multiply(u):
            if not 0 <= u < UNITS:
                return
            b = u // HALVES
            x_codes, x_scales, sq_codes, sq_scales = operands[u]
            m1 = psum.tile([P, DH], F32, tag="m1")
            m2 = psum.tile([P, DH], F32, tag="m2")
            for acc, codes, scales in ((m1, x_codes, x_scales), (m2, sq_codes, sq_scales)):
                for g in range(PASSES):
                    nc.tensor.matmul_mx(
                        out=acc[:],
                        lhsT=p_codes[:, b, g * K : (g + 1) * K].bitcast(FP8X4),
                        lhsT_scale=p_scales[:, b, g * K : (g + 1) * K],
                        rhs=codes[:, g, :].bitcast(FP8X4),
                        rhs_scale=scales[:, g, :],
                        start=(g == 0),
                        stop=(g == PASSES - 1),
                    )
            moments[u] = (m1, m2)

        def square_mean(u):
            if not 0 <= u < UNITS:
                return
            m1_sq = work.tile([P, DH], F32, tag="m1_sq")
            nc.scalar.activation(out=m1_sq[:], in_=moments[u][0][:], func=ACT.Square)
            m1_squares[u] = m1_sq

        def variance(u):
            if not 0 <= u < UNITS:
                return
            b, h = divmod(u, HALVES)
            cols = slice(h * DH, (h + 1) * DH)
            if h == 0:
                feat = work.tile([P, 2, D], F32, tag="feat", bufs=3)
                feats[b] = feat
                sums = small.tile([P, HALVES], F32, tag="sums")
                sums_sq[b] = sums
            m1, m2 = moments[u]
            var = work.tile([P, DH], F32, tag="var")
            nc.vector.tensor_tensor(out=var[:], in0=m2[:], in1=m1_squares[u][:], op=ALU.subtract)
            nc.vector.tensor_tensor(out=feats[b][:, 0, cols], in0=m1[:], in1=mu_t[:, cols], op=ALU.subtract)
            nc.vector.tensor_scalar_max(out=var[:], in0=var[:], scalar1=EPS)
            variances[u] = var

        def deviation(u):
            if not 0 <= u < UNITS:
                return
            b, h = divmod(u, HALVES)
            cols = slice(h * DH, (h + 1) * DH)
            std = work.tile([P, DH], F32, tag="std")
            nc.scalar.activation(out=std[:], in_=variances[u][:], func=ACT.Sqrt)
            nc.vector.tensor_tensor(out=feats[b][:, 1, cols], in0=std[:], in1=sigma_t[:, cols], op=ALU.subtract)

        def close_sums(u):
            if not 0 <= u < UNITS:
                return
            b, h = divmod(u, HALVES)
            unread = work.tile([P, 2, DH], BF16, tag="unread_sq")
            nc.scalar.activation(
                out=unread[:],
                in_=feats[b][:, :, h * DH : (h + 1) * DH],
                func=ACT.Square,
                accum_out=sums_sq[b][:, h : h + 1],
            )

        def closes_batch(u):
            return 0 <= u < UNITS and u % HALVES == HALVES - 1

        def column_norms(u):
            if not closes_batch(u):
                return
            b = u // HALVES
            halves = sums_sq[b]
            floored = small.tile([P, 1], F32, tag="floored")
            nc.vector.tensor_scalar(
                out=floored[:], in0=halves[:, 0:1], scalar1=halves[:, 1:2], scalar2=EPS * EPS, op0=ALU.add, op1=ALU.max
            )
            left_sq = small.tile([P, 1], F32, tag="left_sq")
            nc.vector.tensor_scalar(
                out=left_sq[:], in0=halves[:, 0:1], scalar1=halves[:, 1:2], scalar2=EPS * EPS, op0=ALU.add, op1=ALU.min
            )
            col_norms[b] = (floored, left_sq)

        def spread_left(u):
            if not closes_batch(u):
                return
            b = u // HALVES
            spread = psum.tile([P, 2, P], F32, tag="misc")
            nc.tensor.matmul(
                out=spread[:, 1, 0:1], lhsT=col_norms[b][1][:, 0:1].to_broadcast([P, P]), rhs=ones_f32[:, 0:1],
                start=True, stop=True,
            )
            spreads[b] = spread

        def whole_norm(u):
            if not closes_batch(u):
                return
            b = u // HALVES
            both = small.tile([P, 1], F32, tag="both")
            nc.vector.tensor_scalar(
                out=both[:], in0=spreads[b][:, 1, 0:1], scalar1=EPS**4, scalar2=col_norms[b][0][:, 0:1],
                op0=ALU.max, op1=ALU.mult,
            )
            inv_both = small.tile([P, 1], F32, tag="inv_both")
            nc.vector.reciprocal(out=inv_both[:], in_=both[:])
            inv_alls[b] = inv_both

        def spread_factor(u):
            if not closes_batch(u):
                return
            b = u // HALVES
            nc.tensor.transpose(spreads[b][:, 0, :], inv_alls[b][:, 0:1].to_broadcast([P, P]), ident_f32[:])
            factor = small.tile([P, K], F32, tag="factor")
            nc.scalar.activation(out=factor[:], in_=spreads[b][:, 0, :], func=ACT.Sqrt, scale=EPS * EPS)
            factors[b] = factor

        def turn_back(w):
            if not 0 <= w < UNITS:
                return
            b, s = divmod(w, 2)
            for h in range(HALVES):
                bank = psum.tile([P, TH, K], F32, tag="turn", bufs=TURN_BANKS)
                for i in range(TH):
                    t = h * TH + i
                    nc.tensor.transpose(bank[:, i, :], feats[b][:, s, t * P : (t + 1) * P], ident_f32[:])
                out_banks[(w, h)] = bank

        def scale_and_store(w):
            if not 0 <= w < UNITS:
                return
            b, s = divmod(w, 2)
            for h in range(HALVES):
                result = work.tile([P, TH, K], F32, tag="result", bufs=8)
                nc.vector.tensor_tensor(
                    out=result[:],
                    in0=out_banks[(w, h)][:],
                    in1=factors[b][:].unsqueeze(1).to_broadcast([P, TH, K]),
                    op=ALU.mult,
                )
                nc.sync.dma_start(out=out_view[b, s, :, h * TH : (h + 1) * TH, :], in_=result[:])

        normalise_p(0)
        turn_x(0, 0)
        for b in range(1, B):
            normalise_p(b)
            quantise_p(b - 1)
        quantise_p(B - 1)
        for r in range(UNITS + TURN_LAG):
            u = r - LAG
            w = r - TURN_LAG
            column_norms(u - 1)
            variance(u)
            scale_and_store(w)
            quantise_x(r, 0)
            turn_x(r, 1)
            multiply(u + 1)
            turn_back(w + 1)
            spread_left(u - 1)
            deviation(u)
            quantise_x(r, 1)
            turn_x(r + 1, 0)
            close_sums(u)
            square_mean(u + 1)
            whole_norm(u - 1)
            spread_factor(u - 1)
            if r == 0:
                turn_mu_sigma()
